import numpy as np
import ml_dtypes


def mxq(x, axis, fmt="e4m3"):
    dtype, down = {"e4m3": (ml_dtypes.float8_e4m3fn, 7), "e5m2": (ml_dtypes.float8_e5m2, 14)}[fmt]
    v = np.moveaxis(np.asarray(x, np.float32).astype(ml_dtypes.bfloat16).astype(np.float64), axis, -1)
    blocks = v.reshape(v.shape[:-1] + (-1, 32))
    amax = np.abs(blocks).max(-1, keepdims=True)
    byte = np.maximum(np.where(amax > 0, np.frexp(amax)[1] - 1 + 127, 0) - down, 1)
    scale = np.exp2(byte - 127.0)
    codes = (blocks / scale).astype(np.float32).astype(dtype).astype(np.float64)
    return np.moveaxis((codes * scale).reshape(v.shape), -1, axis)


WIDE = False


def mx_kscale(k):
    if not WIDE:
        return np.ones(k)
    levels = np.array([10, -10, 5, -5, 0])
    a = np.random.permutation(np.resize(levels, k // 512 * 4)).reshape(k // 512, 4)
    idx = np.arange(k)
    return np.exp2(a[idx // 512, idx % 128 // 32])


BF16 = ml_dtypes.bfloat16


def bf(x):
    return np.asarray(x, np.float32).astype(BF16)


def f64(x):
    return np.asarray(x).astype(np.float64)


E2M1 = np.array([0.0, 0.5, 1.0, 1.5, 2.0, 3.0, 4.0, 6.0, -0.0, -0.5, -1.0, -1.5, -2.0, -3.0, -4.0, -6.0])


def pack_weight(w, fmt):
    k, n = w.shape
    w = f64(bf(w)).reshape(k // 32, 32, n)
    amax = np.abs(w).max(1)
    if fmt == "e4m3":
        byte = np.frexp(amax)[1] - 1 + 127 - 7
    else:
        mant, ex = np.frexp(amax / 6.0)
        byte = np.where(mant > 0.5, ex, ex - 1) + 127
    byte = np.clip(np.where(amax > 0, byte, 1), 1, 254)
    scaled = (w * np.exp2(127.0 - byte)[:, None, :]).reshape(k, n).astype(np.float32)
    by_word = np.ascontiguousarray(scaled.reshape(k // 512, 128, 4, n).transpose(0, 1, 3, 2))
    if fmt == "e4m3":
        words = by_word.astype(ml_dtypes.float8_e4m3fn).view(np.uint8)
    else:
        c = by_word.astype(ml_dtypes.float4_e2m1fn).view(np.uint8) & 0xF
        words = c[..., 0::2] | (c[..., 1::2] << 4)
    return np.ascontiguousarray(words), np.ascontiguousarray(byte.astype(np.uint8).reshape(k // 512, 16, n))


def unpack_weight(words, scales, fmt):
    g, p, n, _ = words.shape
    if fmt == "e4m3":
        vals = np.ascontiguousarray(words).view(ml_dtypes.float8_e4m3fn).astype(np.float64)
    else:
        nib = np.empty((g, p, n, 4), np.uint8)
        nib[..., 0::2] = words & 0xF
        nib[..., 1::2] = words >> 4
        vals = E2M1[nib]
    vals = vals * np.repeat(np.exp2(scales.astype(np.float64) - 127.0), 8, axis=1)[..., None]
    return vals.transpose(0, 1, 3, 2).reshape(g * 512, n)


T, B, I, H = 4, 128, 16384, 128
FMT = "e4m3"


def sigmoid(v):
    return 1.0 / (1.0 + np.exp(-v))


def setup_inputs():
    s = mx_kscale(I)
    input_seq = bf(np.random.standard_normal((T, B, I)) * s)
    w = np.random.standard_normal((3 * H, I)) / np.sqrt(I) / s[None, :]
    words, scales = pack_weight(np.ascontiguousarray(w.T), FMT)
    b_ih = bf(np.random.standard_normal(3 * H) * 0.3)
    gh = bf(np.random.standard_normal((B, 3 * H)) * 0.5)
    return {"input_seq": input_seq,
            "W_ih_words": words,
            "W_ih_scales": scales,
            "b_ih": b_ih,
            "gh": gh}


def reference(input_seq, W_ih_words, W_ih_scales, b_ih, gh):
    gi = (mxq(f64(input_seq), 2, "e4m3") @ unpack_weight(W_ih_words, W_ih_scales, FMT)) + f64(b_ih)
    g = f64(gh)
    i_r, i_z, i_n = gi[..., :H], gi[..., H:2 * H], gi[..., 2 * H:]
    h_r, h_z, h_n = g[..., :H], g[..., H:2 * H], g[..., 2 * H:]
    r = sigmoid(i_r + h_r)
    z = sigmoid(i_z + h_z)
    n = np.tanh(i_n + r * h_n)
    h = (1.0 - z) * n
    return np.transpose(h, (1, 0, 2))

@@ -1,0 +1,215 @@
+from contextlib import ExitStack
+
+import concourse.mybir as mybir
+from concourse.masks import make_identity
+
+F32 = mybir.dt.float32
+BF16 = mybir.dt.bfloat16
+I32 = mybir.dt.int32
+U32 = mybir.dt.uint32
+U8 = mybir.dt.uint8
+FP8X4 = mybir.dt.float8_e4m3fn_x4
+ADD = mybir.AluOpType.add
+MULT = mybir.AluOpType.mult
+SIGMOID = mybir.ActivationFunctionType.Sigmoid
+TANH = mybir.ActivationFunctionType.Tanh
+
+P = 128
+T, B, I, H = 4, 128, 16384, 128
+GATES = 3
+ROWS = T * B
+PACK = 4
+K_PASS = P * PACK
+PASSES = I // K_PASS
+HALVES = 2
+WORDS = P * HALVES
+ROUND = 2
+ROUNDS = PASSES // ROUND
+CHUNK = 4
+CHUNKS = PASSES // CHUNK
+ROUNDS_PER_CHUNK = CHUNK // ROUND
+RAW_BUFS = 4
+SORT_AHEAD = 2
+
+FLOPS = 2 * ROWS * I * GATES * H
+
+
+def tile_grucellmodel_pa_k_kernel(tc, input_seq, W_ih_words, W_ih_scales, b_ih, gh, out):
+    nc = tc.nc
+    with ExitStack() as ctx:
+        consts = ctx.enter_context(tc.tile_pool(name="consts", bufs=1))
+        raw_pool = ctx.enter_context(tc.tile_pool(name="raw", bufs=RAW_BUFS))
+        stage = ctx.enter_context(tc.tile_pool(name="stage", bufs=3))
+        tail = ctx.enter_context(tc.tile_pool(name="tail", bufs=1))
+        acc_pool = ctx.enter_context(tc.psum_pool(name="acc", bufs=1))
+        xt_pool = ctx.enter_context(tc.psum_pool(name="xt", bufs=4))
+        misc_pool = ctx.enter_context(tc.psum_pool(name="misc", bufs=1))
+        ctx.enter_context(tc.manual_schedule())
+
+        x_view = input_seq.rearrange("t b k -> b t k")
+        w_view = W_ih_words.rearrange("g p n t -> p g (n t)").bitcast(I32)
+        s_view = W_ih_scales.rearrange("g (q r) n -> r q g n", r=4).bitcast(I32)
+
+        raws = []
+        w_chunks = []
+
+        def load_chunk(c):
+            raw = raw_pool.tile([P, T, CHUNK * K_PASS], BF16)
+            nc.sync.dma_start(out=raw[:], in_=x_view[:, :, c * CHUNK * K_PASS : (c + 1) * CHUNK * K_PASS])
+            raws.append(raw)
+
+        def load_weights(c):
+            w_chunk = consts.tile([P, CHUNK, GATES * H], I32, name="w_chunk%d" % c, align_bytes=64)
+            nc.sync.dma_start(out=w_chunk[:], in_=w_view[:, c * CHUNK : (c + 1) * CHUNK, :])
+            w_chunks.append(w_chunk)
+
+        w_planes = consts.tile([P, PASSES, GATES * H], U8, align_bytes=64)
+        nc.vector.memset(w_planes[:].bitcast(I32), 0)
+
+        small_bf = consts.tile([P, (GATES + 1) * H], BF16)
+        nc.vector.memset(small_bf[:, GATES * H :], 0.0)
+        nc.scalar.dma_start(out=small_bf[:, : GATES * H], in_=gh)
+        nc.scalar.dma_start(out=small_bf[0:GATES, GATES * H :], in_=b_ih.rearrange("(g h) -> g h", g=GATES))
+
+        warm_in = consts.tile([P, 1], F32)
+        warm_out = consts.tile([P, 1], F32)
+        nc.vector.memset(warm_in[:], 0.0)
+        nc.scalar.activation(out=warm_out[:], in_=warm_in[:], func=SIGMOID)
+
+        ident = consts.tile([P, P], F32)
+        make_identity(nc, ident[:])
+
+        load_chunk(0)
+        for r in range(4):
+            nc.sync.dma_start(out=w_planes[r:P:32, :, :].bitcast(I32), in_=s_view[r])
+        load_weights(0)
+        for c in range(1, RAW_BUFS):
+            load_chunk(c)
+            load_weights(c)
+
+        small_f = consts.tile([P, GATES + 1, H], F32)
+        nc.vector.tensor_copy(out=small_f[:].rearrange("p g h -> p (g h)"), in_=small_bf[:])
+        small_ps = misc_pool.tile([P, GATES + 1, B], F32, tag="misc")
+        for j in range(GATES + 1):
+            nc.tensor.transpose(out=small_ps[:, j, :], in_=small_f[:, j, :], identity=ident[:])
+        ghT = consts.tile([P, GATES + 1, B], F32)
+        nc.vector.tensor_copy(out=ghT[:], in_=small_ps[:])
+        bias_r = ghT[:, GATES, 0:1]
+        bias_z = ghT[:, GATES, 1:2]
+        bias_n = ghT[:, GATES, 2:3]
+        gh_bias = consts.tile([P, 2, B], F32)
+        nc.vector.tensor_scalar_add(out=gh_bias[:, 0, :], in0=ghT[:, 0, :], scalar1=bias_r)
+        nc.vector.tensor_scalar_add(out=gh_bias[:, 1, :], in0=ghT[:, 1, :], scalar1=bias_z)
+
+        acc = [acc_pool.tile([P, ROWS], F32, name="acc%d" % gate) for gate in range(GATES)]
+
+        sorted_tiles = {}
+        bank_tiles = {}
+        code_tiles = {}
+
+        def sort_words(r):
+            raw32 = raws[r // ROUNDS_PER_CHUNK][:].bitcast(F32)
+            lo = (r % ROUNDS_PER_CHUNK) * ROUND * WORDS
+            srt = stage.tile([P, T, ROUND, HALVES, P], F32)
+            nc.vector.tensor_copy(
+                out=srt[:],
+                in_=raw32[:, :, lo : lo + ROUND * WORDS].rearrange("b t (g p u) -> b t g u p", g=ROUND, u=HALVES),
+            )
+            sorted_tiles[r] = srt
+
+        def transposes(r):
+            srt = sorted_tiles[r]
+            banks = []
+            for g in range(ROUND):
+                for pair in range(T // 2):
+                    xt = xt_pool.tile([P, 2 * HALVES, B], F32)
+                    for t in range(2):
+                        for u in range(HALVES):
+                            nc.tensor.transpose(
+                                out=xt[:, t * HALVES + u, :], in_=srt[:, 2 * pair + t, g, u, :], identity=ident[:]
+                            )
+                    banks.append(xt)
+            bank_tiles[r] = banks
+
+        def quantise(r):
+            grouped = stage.tile([P, ROUND, ROWS * PACK], BF16, align_bytes=64)
+            codes = stage.tile([P, ROUND, ROWS], U32, align_bytes=64)
+            x_planes = stage.tile([P, ROUND, ROWS], U8, align_bytes=64)
+            grouped32 = grouped[:].bitcast(F32)
+            span = 2 * B * HALVES
+            for g in range(ROUND):
+                for pair in range(T // 2):
+                    nc.scalar.copy(
+                        out=grouped32[:, g, pair * span : (pair + 1) * span].rearrange(
+                            "p (t b u) -> p t b u", t=2, u=HALVES
+                        ),
+                        in_=bank_tiles[r][g * (T // 2) + pair][:].rearrange("p (t u) b -> p t b u", u=HALVES),
+                    )
+                nc.vector.quantize_mx(
+                    out=codes[:, g, :].bitcast(FP8X4), scales=x_planes[:, g, :], in_=grouped[:, g, :]
+                )
+            code_tiles[r] = (codes, x_planes)
+
+        def passes(r):
+            codes, x_planes = code_tiles[r]
+            for gate in range(GATES):
+                cols = slice(gate * H, (gate + 1) * H)
+                for g in range(ROUND):
+                    k_pass = r * ROUND + g
+                    nc.tensor.matmul_mx(
+                        out=acc[gate][:],
+                        lhsT=w_chunks[k_pass // CHUNK][:, k_pass % CHUNK, cols].bitcast(FP8X4),
+                        lhsT_scale=w_planes[:, k_pass, cols],
+                        rhs=codes[:, g, :].bitcast(FP8X4),
+                        rhs_scale=x_planes[:, g, :],
+                        start=(k_pass == 0),
+                        stop=(k_pass == PASSES - 1),
+                    )
+
+        def sort_and_refill(r):
+            sort_words(r)
+            c = r // ROUNDS_PER_CHUNK + RAW_BUFS
+            if r % ROUNDS_PER_CHUNK == ROUNDS_PER_CHUNK - 1 and c < CHUNKS:
+                load_chunk(c)
+                load_weights(c)
+
+        for r in range(SORT_AHEAD):
+            sort_and_refill(r)
+        for r in range(ROUNDS):
+            if r + SORT_AHEAD < ROUNDS:
+                sort_and_refill(r + SORT_AHEAD)
+            transposes(r)
+            quantise(r)
+            if r > 0:
+                passes(r - 1)
+        passes(ROUNDS - 1)
+
+        def by_step(ap):
+            return ap.rearrange("p (t b) -> p t b", t=T)
+
+        def every_step(ap):
+            return ap.unsqueeze(1).to_broadcast([P, T, B])
+
+        pre_r = tail.tile([P, T, B], F32)
+        nc.vector.tensor_tensor(out=pre_r[:], in0=by_step(acc[0][:]), in1=every_step(gh_bias[:, 0, :]), op=ADD)
+        r_gate = tail.tile([P, T, B], F32)
+        nc.scalar.activation(out=r_gate[:], in_=pre_r[:], func=SIGMOID)
+        pre_z = tail.tile([P, T, B], F32)
+        nc.vector.tensor_tensor(out=pre_z[:], in0=by_step(acc[1][:]), in1=every_step(gh_bias[:, 1, :]), op=ADD)
+        one_minus_z = tail.tile([P, T, B], F32)
+        nc.scalar.activation(out=one_minus_z[:], in_=pre_z[:], func=SIGMOID, scale=-1.0)
+        r_hn = tail.tile([P, T, B], F32)
+        nc.vector.tensor_tensor(out=r_hn[:], in0=r_gate[:], in1=every_step(ghT[:, 2, :]), op=MULT)
+        pre_n = tail.tile([P, T, B], F32)
+        nc.vector.tensor_tensor(out=pre_n[:], in0=by_step(acc[2][:]), in1=r_hn[:], op=ADD)
+        n_gate = tail.tile([P, T, B], F32)
+        nc.scalar.activation(out=n_gate[:], in_=pre_n[:], func=TANH, bias=bias_n)
+        h_new = tail.tile([P, T, B], F32)
+        nc.vector.tensor_tensor(out=h_new[:], in0=one_minus_z[:], in1=n_gate[:], op=MULT)
+
+        h_ps = misc_pool.tile([P, T, H], F32, tag="misc")
+        for t in range(T):
+            nc.tensor.transpose(out=h_ps[:, t, :], in_=h_new[:, t, :], identity=ident[:])
+        h_out = tail.tile([P, T, H], F32)
+        nc.vector.tensor_copy(out=h_out[:], in_=h_ps[:])
+        nc.sync.dma_start(out=out, in_=h_out[:])

@@ -29,7 +29,9 @@ CHUNK = 4
 CHUNKS = PASSES // CHUNK
 ROUNDS_PER_CHUNK = CHUNK // ROUND
 RAW_BUFS = 4
-SORT_AHEAD = 2
+SORT_AHEAD = 1
+XT_BANKS = 5
+STEPS = 2
 
 FLOPS = 2 * ROWS * I * GATES * H
 
@@ -42,8 +44,7 @@ def tile_grucellmodel_pa_k_kernel(tc, input_seq, W_ih_words, W_ih_scales, b_ih, 
         stage = ctx.enter_context(tc.tile_pool(name="stage", bufs=3))
         tail = ctx.enter_context(tc.tile_pool(name="tail", bufs=1))
         acc_pool = ctx.enter_context(tc.psum_pool(name="acc", bufs=1))
-        xt_pool = ctx.enter_context(tc.psum_pool(name="xt", bufs=4))
-        misc_pool = ctx.enter_context(tc.psum_pool(name="misc", bufs=1))
+        xt_pool = ctx.enter_context(tc.psum_pool(name="xt", bufs=XT_BANKS))
         ctx.enter_context(tc.manual_schedule())
 
         x_view = input_seq.rearrange("t b k -> b t k")
@@ -89,7 +90,7 @@ def tile_grucellmodel_pa_k_kernel(tc, input_seq, W_ih_words, W_ih_scales, b_ih, 
 
         small_f = consts.tile([P, GATES + 1, H], F32)
         nc.vector.tensor_copy(out=small_f[:].rearrange("p g h -> p (g h)"), in_=small_bf[:])
-        small_ps = misc_pool.tile([P, GATES + 1, B], F32, tag="misc")
+        small_ps = xt_pool.tile([P, GATES + 1, B], F32, tag="xt")
         for j in range(GATES + 1):
             nc.tensor.transpose(out=small_ps[:, j, :], in_=small_f[:, j, :], identity=ident[:])
         ghT = consts.tile([P, GATES + 1, B], F32)
@@ -122,7 +123,7 @@ def tile_grucellmodel_pa_k_kernel(tc, input_seq, W_ih_words, W_ih_scales, b_ih, 
             banks = []
             for g in range(ROUND):
                 for pair in range(T // 2):
-                    xt = xt_pool.tile([P, 2 * HALVES, B], F32)
+                    xt = xt_pool.tile([P, 2 * HALVES, B], F32, tag="xt")
                     for t in range(2):
                         for u in range(HALVES):
                             nc.tensor.transpose(
@@ -184,32 +185,35 @@ def tile_grucellmodel_pa_k_kernel(tc, input_seq, W_ih_words, W_ih_scales, b_ih, 
                 passes(r - 1)
         passes(ROUNDS - 1)
 
-        def by_step(ap):
-            return ap.rearrange("p (t b) -> p t b", t=T)
+        pieces = range(T // STEPS)
+
+        def sums(gate, piece):
+            return acc[gate][:, piece * STEPS * B : (piece + 1) * STEPS * B].rearrange("p (t b) -> p t b", t=STEPS)
 
         def every_step(ap):
-            return ap.unsqueeze(1).to_broadcast([P, T, B])
+            return ap.unsqueeze(1).to_broadcast([P, STEPS, B])
 
-        pre_r = tail.tile([P, T, B], F32)
-        nc.vector.tensor_tensor(out=pre_r[:], in0=by_step(acc[0][:]), in1=every_step(gh_bias[:, 0, :]), op=ADD)
-        r_gate = tail.tile([P, T, B], F32)
-        nc.scalar.activation(out=r_gate[:], in_=pre_r[:], func=SIGMOID)
-        pre_z = tail.tile([P, T, B], F32)
-        nc.vector.tensor_tensor(out=pre_z[:], in0=by_step(acc[1][:]), in1=every_step(gh_bias[:, 1, :]), op=ADD)
-        one_minus_z = tail.tile([P, T, B], F32)
-        nc.scalar.activation(out=one_minus_z[:], in_=pre_z[:], func=SIGMOID, scale=-1.0)
-        r_hn = tail.tile([P, T, B], F32)
-        nc.vector.tensor_tensor(out=r_hn[:], in0=r_gate[:], in1=every_step(ghT[:, 2, :]), op=MULT)
-        pre_n = tail.tile([P, T, B], F32)
-        nc.vector.tensor_tensor(out=pre_n[:], in0=by_step(acc[2][:]), in1=r_hn[:], op=ADD)
-        n_gate = tail.tile([P, T, B], F32)
-        nc.scalar.activation(out=n_gate[:], in_=pre_n[:], func=TANH, bias=bias_n)
-        h_new = tail.tile([P, T, B], F32)
-        nc.vector.tensor_tensor(out=h_new[:], in0=one_minus_z[:], in1=n_gate[:], op=MULT)
+        def tail_tiles(name):
+            return [tail.tile([P, STEPS, B], F32, name="%s%d" % (name, piece)) for piece in pieces]
 
-        h_ps = misc_pool.tile([P, T, H], F32, tag="misc")
-        for t in range(T):
-            nc.tensor.transpose(out=h_ps[:, t, :], in_=h_new[:, t, :], identity=ident[:])
-        h_out = tail.tile([P, T, H], F32)
-        nc.vector.tensor_copy(out=h_out[:], in_=h_ps[:])
-        nc.sync.dma_start(out=out, in_=h_out[:])
+        pre_r, r_gate, pre_z, one_minus_z = tail_tiles("pre_r"), tail_tiles("r_gate"), tail_tiles("pre_z"), tail_tiles("omz")
+        r_hn, pre_n, n_gate, h_new, h_out = (
+            tail_tiles("r_hn"), tail_tiles("pre_n"), tail_tiles("n_gate"), tail_tiles("h_new"), tail_tiles("h_out")
+        )
+        for i in pieces:
+            nc.vector.tensor_tensor(out=pre_r[i][:], in0=sums(0, i), in1=every_step(gh_bias[:, 0, :]), op=ADD)
+            nc.scalar.activation(out=r_gate[i][:], in_=pre_r[i][:], func=SIGMOID)
+        for i in pieces:
+            nc.vector.tensor_tensor(out=pre_z[i][:], in0=sums(1, i), in1=every_step(gh_bias[:, 1, :]), op=ADD)
+            nc.scalar.activation(out=one_minus_z[i][:], in_=pre_z[i][:], func=SIGMOID, scale=-1.0)
+        for i in pieces:
+            nc.vector.tensor_tensor(out=r_hn[i][:], in0=r_gate[i][:], in1=every_step(ghT[:, 2, :]), op=MULT)
+            nc.vector.tensor_tensor(out=pre_n[i][:], in0=sums(2, i), in1=r_hn[i][:], op=ADD)
+            nc.scalar.activation(out=n_gate[i][:], in_=pre_n[i][:], func=TANH, bias=bias_n)
+        for i in pieces:
+            nc.vector.tensor_tensor(out=h_new[i][:], in0=one_minus_z[i][:], in1=n_gate[i][:], op=MULT)
+            h_ps = xt_pool.tile([P, STEPS, H], F32, tag="xt")
+            for t in range(STEPS):
+                nc.tensor.transpose(out=h_ps[:, t, :], in_=h_new[i][:, t, :], identity=ident[:])
+            nc.scalar.copy(out=h_out[i][:], in_=h_ps[:])
+            nc.sync.dma_start(out=out[:, i * STEPS : (i + 1) * STEPS, :], in_=h_out[i][:])

@@ -65,10 +65,9 @@ def tile_grucellmodel_pa_k_kernel(tc, input_seq, W_ih_words, W_ih_scales, b_ih, 
             w_chunks.append(w_chunk)
 
         w_planes = consts.tile([P, PASSES, GATES * H], U8, align_bytes=64)
-        nc.vector.memset(w_planes[:].bitcast(I32), 0)
-
         small_bf = consts.tile([P, (GATES + 1) * H], BF16)
         nc.vector.memset(small_bf[:, GATES * H :], 0.0)
+        nc.vector.memset(w_planes[:].bitcast(I32), 0)
         nc.scalar.dma_start(out=small_bf[:, : GATES * H], in_=gh)
         nc.scalar.dma_start(out=small_bf[0:GATES, GATES * H :], in_=b_ih.rearrange("(g h) -> g h", g=GATES))
 
@@ -197,23 +196,30 @@ def tile_grucellmodel_pa_k_kernel(tc, input_seq, W_ih_words, W_ih_scales, b_ih, 
             return [tail.tile([P, STEPS, B], F32, name="%s%d" % (name, piece)) for piece in pieces]
 
         pre_r, r_gate, pre_z, one_minus_z = tail_tiles("pre_r"), tail_tiles("r_gate"), tail_tiles("pre_z"), tail_tiles("omz")
-        r_hn, pre_n, n_gate, h_new, h_out = (
-            tail_tiles("r_hn"), tail_tiles("pre_n"), tail_tiles("n_gate"), tail_tiles("h_new"), tail_tiles("h_out")
+        r_hn, pre_n, n_gate, omz_rows, h_out = (
+            tail_tiles("r_hn"), tail_tiles("pre_n"), tail_tiles("n_gate"), tail_tiles("omz_rows"), tail_tiles("h_out")
         )
+
+        def to_rows(values):
+            rows = xt_pool.tile([P, STEPS, H], F32, tag="xt")
+            for t in range(STEPS):
+                nc.tensor.transpose(out=rows[:, t, :], in_=values[:, t, :], identity=ident[:])
+            return rows
+
         for i in pieces:
             nc.vector.tensor_tensor(out=pre_r[i][:], in0=sums(0, i), in1=every_step(gh_bias[:, 0, :]), op=ADD)
             nc.scalar.activation(out=r_gate[i][:], in_=pre_r[i][:], func=SIGMOID)
         for i in pieces:
             nc.vector.tensor_tensor(out=pre_z[i][:], in0=sums(1, i), in1=every_step(gh_bias[:, 1, :]), op=ADD)
             nc.scalar.activation(out=one_minus_z[i][:], in_=pre_z[i][:], func=SIGMOID, scale=-1.0)
+        omz_banks = [to_rows(one_minus_z[i]) for i in pieces]
         for i in pieces:
             nc.vector.tensor_tensor(out=r_hn[i][:], in0=r_gate[i][:], in1=every_step(ghT[:, 2, :]), op=MULT)
             nc.vector.tensor_tensor(out=pre_n[i][:], in0=sums(2, i), in1=r_hn[i][:], op=ADD)
             nc.scalar.activation(out=n_gate[i][:], in_=pre_n[i][:], func=TANH, bias=bias_n)
+        nc.vector.tensor_copy(out=omz_rows[0][:], in_=omz_banks[0][:])
+        nc.scalar.copy(out=omz_rows[1][:], in_=omz_banks[1][:])
         for i in pieces:
-            nc.vector.tensor_tensor(out=h_new[i][:], in0=one_minus_z[i][:], in1=n_gate[i][:], op=MULT)
-            h_ps = xt_pool.tile([P, STEPS, H], F32, tag="xt")
-            for t in range(STEPS):
-                nc.tensor.transpose(out=h_ps[:, t, :], in_=h_new[i][:, t, :], identity=ident[:])
-            nc.scalar.copy(out=h_out[i][:], in_=h_ps[:])
+            n_rows = to_rows(n_gate[i])
+            nc.vector.tensor_tensor(out=h_out[i][:], in0=n_rows[:], in1=omz_rows[i][:], op=MULT)
             nc.sync.dma_start(out=out[:, i * STEPS : (i + 1) * STEPS, :], in_=h_out[i][:])

@@ -25,12 +25,14 @@ HALVES = 2
 WORDS = P * HALVES
 ROUND = 2
 ROUNDS = PASSES // ROUND
-CHUNK = 4
-CHUNKS = PASSES // CHUNK
-ROUNDS_PER_CHUNK = CHUNK // ROUND
-RAW_BUFS = 4
+LOAD_ROUNDS = (3, 2, 2, 2, 2, 2, 2, 1)
+LOADS = len(LOAD_ROUNDS)
+W_ROUNDS = 2
+SLOT_OF = {3: 3, 2: 2, 1: 2}
+RAW_BUFS = {3: 1, 2: 4}
 SORT_AHEAD = 1
 XT_BANKS = 5
+TAIL_TILES = 18
 STEPS = 2
 
 FLOPS = 2 * ROWS * I * GATES * H
@@ -38,11 +40,12 @@ FLOPS = 2 * ROWS * I * GATES * H
 
 def tile_grucellmodel_pa_k_kernel(tc, input_seq, W_ih_words, W_ih_scales, b_ih, gh, out):
     nc = tc.nc
+    LOAD_START = [sum(LOAD_ROUNDS[:c]) for c in range(LOADS)]
+    LOAD_OF_ROUND = [c for c in range(LOADS) for i in range(LOAD_ROUNDS[c])]
     with ExitStack() as ctx:
         consts = ctx.enter_context(tc.tile_pool(name="consts", bufs=1))
-        raw_pool = ctx.enter_context(tc.tile_pool(name="raw", bufs=RAW_BUFS))
+        raw_pool = ctx.enter_context(tc.tile_pool(name="raw", bufs=1))
         stage = ctx.enter_context(tc.tile_pool(name="stage", bufs=3))
-        tail = ctx.enter_context(tc.tile_pool(name="tail", bufs=1))
         acc_pool = ctx.enter_context(tc.psum_pool(name="acc", bufs=1))
         xt_pool = ctx.enter_context(tc.psum_pool(name="xt", bufs=XT_BANKS))
         ctx.enter_context(tc.manual_schedule())
@@ -51,18 +54,22 @@ def tile_grucellmodel_pa_k_kernel(tc, input_seq, W_ih_words, W_ih_scales, b_ih, 
         w_view = W_ih_words.rearrange("g p n t -> p g (n t)").bitcast(I32)
         s_view = W_ih_scales.rearrange("g (q r) n -> r q g n", r=4).bitcast(I32)
 
-        raws = []
-        w_chunks = []
+        raws = {}
+        w_tiles = {}
 
-        def load_chunk(c):
-            raw = raw_pool.tile([P, T, CHUNK * K_PASS], BF16)
-            nc.sync.dma_start(out=raw[:], in_=x_view[:, :, c * CHUNK * K_PASS : (c + 1) * CHUNK * K_PASS])
-            raws.append(raw)
+        def load_x(c):
+            n = LOAD_ROUNDS[c]
+            lo = LOAD_START[c] * ROUND * K_PASS
+            raw = raw_pool.tile([P, T, n * ROUND * K_PASS], BF16, tag="raw%d" % SLOT_OF[n], bufs=RAW_BUFS[SLOT_OF[n]])
+            nc.sync.dma_start(out=raw[:], in_=x_view[:, :, lo : lo + n * ROUND * K_PASS])
+            raws[c] = raw
 
-        def load_weights(c):
-            w_chunk = consts.tile([P, CHUNK, GATES * H], I32, name="w_chunk%d" % c, align_bytes=64)
-            nc.sync.dma_start(out=w_chunk[:], in_=w_view[:, c * CHUNK : (c + 1) * CHUNK, :])
-            w_chunks.append(w_chunk)
+        def load_w(c):
+            n = W_ROUNDS * ROUND
+            lo = c * n
+            w_tile = consts.tile([P, n, GATES * H], I32, name="w_tile%d" % c, align_bytes=64)
+            nc.sync.dma_start(out=w_tile[:], in_=w_view[:, lo : lo + n, :])
+            w_tiles[c] = w_tile
 
         w_planes = consts.tile([P, PASSES, GATES * H], U8, align_bytes=64)
         small_bf = consts.tile([P, (GATES + 1) * H], BF16)
@@ -79,27 +86,61 @@ def tile_grucellmodel_pa_k_kernel(tc, input_seq, W_ih_words, W_ih_scales, b_ih, 
         ident = consts.tile([P, P], F32)
         make_identity(nc, ident[:])
 
-        load_chunk(0)
-        for r in range(4):
-            nc.sync.dma_start(out=w_planes[r:P:32, :, :].bitcast(I32), in_=s_view[r])
-        load_weights(0)
-        for c in range(1, RAW_BUFS):
-            load_chunk(c)
-            load_weights(c)
+        def load_scales():
+            for r in range(4):
+                nc.sync.dma_start(out=w_planes[r:P:32, :, :].bitcast(I32), in_=s_view[r])
+
+        queue = []
+        for c in range(LOADS):
+            queue.append(("x", c))
+            if c == 0:
+                queue.append(("s", 0))
+            queue.append(("w", c))
+        same_slot = {n: [c for c in range(LOADS) if SLOT_OF[LOAD_ROUNDS[c]] == n] for n in RAW_BUFS}
+
+        def rounds_needed(c):
+            peers = same_slot[SLOT_OF[LOAD_ROUNDS[c]]]
+            i = peers.index(c) - RAW_BUFS[SLOT_OF[LOAD_ROUNDS[c]]]
+            return 0 if i < 0 else LOAD_START[peers[i]] + LOAD_ROUNDS[peers[i]]
+
+        def issue_loads(rounds_sorted):
+            while queue and (queue[0][0] != "x" or rounds_needed(queue[0][1]) <= rounds_sorted):
+                kind, c = queue[0]
+                queue.remove(queue[0])
+                if kind == "x":
+                    load_x(c)
+                elif kind == "w":
+                    load_w(c)
+                else:
+                    load_scales()
+
+        issue_loads(0)
 
         small_f = consts.tile([P, GATES + 1, H], F32)
-        nc.vector.tensor_copy(out=small_f[:].rearrange("p g h -> p (g h)"), in_=small_bf[:])
-        small_ps = xt_pool.tile([P, GATES + 1, B], F32, tag="xt")
-        for j in range(GATES + 1):
-            nc.tensor.transpose(out=small_ps[:, j, :], in_=small_f[:, j, :], identity=ident[:])
         ghT = consts.tile([P, GATES + 1, B], F32)
-        nc.vector.tensor_copy(out=ghT[:], in_=small_ps[:])
+        gh_bias = consts.tile([P, 2, B], F32)
         bias_r = ghT[:, GATES, 0:1]
         bias_z = ghT[:, GATES, 1:2]
         bias_n = ghT[:, GATES, 2:3]
-        gh_bias = consts.tile([P, 2, B], F32)
-        nc.vector.tensor_scalar_add(out=gh_bias[:, 0, :], in0=ghT[:, 0, :], scalar1=bias_r)
-        nc.vector.tensor_scalar_add(out=gh_bias[:, 1, :], in0=ghT[:, 1, :], scalar1=bias_z)
+        small_banks = []
+
+        def small_cast():
+            nc.vector.tensor_copy(out=small_f[:].rearrange("p g h -> p (g h)"), in_=small_bf[:])
+
+        def small_transposes():
+            small_ps = xt_pool.tile([P, GATES + 1, B], F32, tag="xt")
+            for j in range(GATES + 1):
+                nc.tensor.transpose(out=small_ps[:, j, :], in_=small_f[:, j, :], identity=ident[:])
+            small_banks.append(small_ps)
+
+        def small_finish():
+            nc.vector.tensor_copy(out=ghT[:], in_=small_banks[0][:])
+            nc.vector.tensor_scalar_add(out=gh_bias[:, 0, :], in0=ghT[:, 0, :], scalar1=bias_r)
+            nc.vector.tensor_scalar_add(out=gh_bias[:, 1, :], in0=ghT[:, 1, :], scalar1=bias_z)
+
+        small_cast()
+        small_transposes()
+        small_finish()
 
         acc = [acc_pool.tile([P, ROWS], F32, name="acc%d" % gate) for gate in range(GATES)]
 
@@ -108,8 +149,9 @@ def tile_grucellmodel_pa_k_kernel(tc, input_seq, W_ih_words, W_ih_scales, b_ih, 
         code_tiles = {}
 
         def sort_words(r):
-            raw32 = raws[r // ROUNDS_PER_CHUNK][:].bitcast(F32)
-            lo = (r % ROUNDS_PER_CHUNK) * ROUND * WORDS
+            c = LOAD_OF_ROUND[r]
+            raw32 = raws[c][:].bitcast(F32)
+            lo = (r - LOAD_START[c]) * ROUND * WORDS
             srt = stage.tile([P, T, ROUND, HALVES, P], F32)
             nc.vector.tensor_copy(
                 out=srt[:],
@@ -158,7 +200,7 @@ def tile_grucellmodel_pa_k_kernel(tc, input_seq, W_ih_words, W_ih_scales, b_ih, 
                     k_pass = r * ROUND + g
                     nc.tensor.matmul_mx(
                         out=acc[gate][:],
-                        lhsT=w_chunks[k_pass // CHUNK][:, k_pass % CHUNK, cols].bitcast(FP8X4),
+                        lhsT=w_tiles[r // W_ROUNDS][:, k_pass % (W_ROUNDS * ROUND), cols].bitcast(FP8X4),
                         lhsT_scale=w_planes[:, k_pass, cols],
                         rhs=codes[:, g, :].bitcast(FP8X4),
                         rhs_scale=x_planes[:, g, :],
@@ -168,10 +210,7 @@ def tile_grucellmodel_pa_k_kernel(tc, input_seq, W_ih_words, W_ih_scales, b_ih, 
 
         def sort_and_refill(r):
             sort_words(r)
-            c = r // ROUNDS_PER_CHUNK + RAW_BUFS
-            if r % ROUNDS_PER_CHUNK == ROUNDS_PER_CHUNK - 1 and c < CHUNKS:
-                load_chunk(c)
-                load_weights(c)
+            issue_loads(r + 1)
 
         for r in range(SORT_AHEAD):
             sort_and_refill(r)
@@ -192,8 +231,15 @@ def tile_grucellmodel_pa_k_kernel(tc, input_seq, W_ih_words, W_ih_scales, b_ih, 
         def every_step(ap):
             return ap.unsqueeze(1).to_broadcast([P, STEPS, B])
 
+        tail_all = raw_pool.tile([P, TAIL_TILES, STEPS, B], F32, tag="raw3", bufs=RAW_BUFS[3])
+        tail_used = []
+
         def tail_tiles(name):
-            return [tail.tile([P, STEPS, B], F32, name="%s%d" % (name, piece)) for piece in pieces]
+            tiles = []
+            for piece in pieces:
+                tiles.append(tail_all[:, len(tail_used), :, :])
+                tail_used.append(name)
+            return tiles
 
         pre_r, r_gate, pre_z, one_minus_z = tail_tiles("pre_r"), tail_tiles("r_gate"), tail_tiles("pre_z"), tail_tiles("omz")
         r_hn, pre_n, n_gate, omz_rows, h_out = (

from contextlib import ExitStack

import concourse.mybir as mybir
from concourse.masks import make_identity

F32 = mybir.dt.float32
BF16 = mybir.dt.bfloat16
I32 = mybir.dt.int32
U32 = mybir.dt.uint32
U8 = mybir.dt.uint8
FP8X4 = mybir.dt.float8_e4m3fn_x4
ADD = mybir.AluOpType.add
MULT = mybir.AluOpType.mult
SIGMOID = mybir.ActivationFunctionType.Sigmoid
TANH = mybir.ActivationFunctionType.Tanh

P = 128
T, B, I, H = 4, 128, 16384, 128
GATES = 3
ROWS = T * B
PACK = 4
K_PASS = P * PACK
PASSES = I // K_PASS
HALVES = 2
WORDS = P * HALVES
ROUND = 2
ROUNDS = PASSES // ROUND
LOAD_ROUNDS = (3, 2, 2, 2, 2, 2, 2, 1)
LOADS = len(LOAD_ROUNDS)
W_ROUNDS = 2
SLOT_OF = {3: 3, 2: 2, 1: 2}
RAW_BUFS = {3: 1, 2: 4}
SORT_AHEAD = 1
XT_BANKS = 5
TAIL_TILES = 18
STEPS = 2

FLOPS = 2 * ROWS * I * GATES * H


def tile_grucellmodel_pa_k_kernel(tc, input_seq, W_ih_words, W_ih_scales, b_ih, gh, out):
    nc = tc.nc
    LOAD_START = [sum(LOAD_ROUNDS[:c]) for c in range(LOADS)]
    LOAD_OF_ROUND = [c for c in range(LOADS) for i in range(LOAD_ROUNDS[c])]
    with ExitStack() as ctx:
        consts = ctx.enter_context(tc.tile_pool(name="consts", bufs=1))
        raw_pool = ctx.enter_context(tc.tile_pool(name="raw", bufs=1))
        stage = ctx.enter_context(tc.tile_pool(name="stage", bufs=3))
        acc_pool = ctx.enter_context(tc.psum_pool(name="acc", bufs=1))
        xt_pool = ctx.enter_context(tc.psum_pool(name="xt", bufs=XT_BANKS))
        ctx.enter_context(tc.manual_schedule())

        x_view = input_seq.rearrange("t b k -> b t k")
        w_view = W_ih_words.rearrange("g p n t -> p g (n t)").bitcast(I32)
        s_view = W_ih_scales.rearrange("g (q r) n -> r q g n", r=4).bitcast(I32)

        raws = {}
        w_tiles = {}

        def load_x(c):
            n = LOAD_ROUNDS[c]
            lo = LOAD_START[c] * ROUND * K_PASS
            raw = raw_pool.tile([P, T, n * ROUND * K_PASS], BF16, tag="raw%d" % SLOT_OF[n], bufs=RAW_BUFS[SLOT_OF[n]])
            nc.sync.dma_start(out=raw[:], in_=x_view[:, :, lo : lo + n * ROUND * K_PASS])
            raws[c] = raw

        def load_w(c):
            n = W_ROUNDS * ROUND
            lo = c * n
            w_tile = consts.tile([P, n, GATES * H], I32, name="w_tile%d" % c, align_bytes=64)
            nc.sync.dma_start(out=w_tile[:], in_=w_view[:, lo : lo + n, :])
            w_tiles[c] = w_tile

        w_planes = consts.tile([P, PASSES, GATES * H], U8, align_bytes=64)
        small_bf = consts.tile([P, (GATES + 1) * H], BF16)
        nc.vector.memset(small_bf[:, GATES * H :], 0.0)
        nc.vector.memset(w_planes[:].bitcast(I32), 0)
        nc.scalar.dma_start(out=small_bf[:, : GATES * H], in_=gh)
        nc.scalar.dma_start(out=small_bf[0:GATES, GATES * H :], in_=b_ih.rearrange("(g h) -> g h", g=GATES))

        warm_in = consts.tile([P, 1], F32)
        warm_out = consts.tile([P, 1], F32)
        nc.vector.memset(warm_in[:], 0.0)
        nc.scalar.activation(out=warm_out[:], in_=warm_in[:], func=SIGMOID)

        ident = consts.tile([P, P], F32)
        make_identity(nc, ident[:])

        def load_scales():
            for r in range(4):
                nc.sync.dma_start(out=w_planes[r:P:32, :, :].bitcast(I32), in_=s_view[r])

        queue = []
        for c in range(LOADS):
            queue.append(("x", c))
            if c == 0:
                queue.append(("s", 0))
            queue.append(("w", c))
        same_slot = {n: [c for c in range(LOADS) if SLOT_OF[LOAD_ROUNDS[c]] == n] for n in RAW_BUFS}

        def rounds_needed(c):
            peers = same_slot[SLOT_OF[LOAD_ROUNDS[c]]]
            i = peers.index(c) - RAW_BUFS[SLOT_OF[LOAD_ROUNDS[c]]]
            return 0 if i < 0 else LOAD_START[peers[i]] + LOAD_ROUNDS[peers[i]]

        def issue_loads(rounds_sorted):
            while queue and (queue[0][0] != "x" or rounds_needed(queue[0][1]) <= rounds_sorted):
                kind, c = queue[0]
                queue.remove(queue[0])
                if kind == "x":
                    load_x(c)
                elif kind == "w":
                    load_w(c)
                else:
                    load_scales()

        issue_loads(0)

        small_f = consts.tile([P, GATES + 1, H], F32)
        ghT = consts.tile([P, GATES + 1, B], F32)
        gh_bias = consts.tile([P, 2, B], F32)
        bias_r = ghT[:, GATES, 0:1]
        bias_z = ghT[:, GATES, 1:2]
        bias_n = ghT[:, GATES, 2:3]
        small_banks = []

        def small_cast():
            nc.vector.tensor_copy(out=small_f[:].rearrange("p g h -> p (g h)"), in_=small_bf[:])

        def small_transposes():
            small_ps = xt_pool.tile([P, GATES + 1, B], F32, tag="xt")
            for j in range(GATES + 1):
                nc.tensor.transpose(out=small_ps[:, j, :], in_=small_f[:, j, :], identity=ident[:])
            small_banks.append(small_ps)

        def small_finish():
            nc.vector.tensor_copy(out=ghT[:], in_=small_banks[0][:])
            nc.vector.tensor_scalar_add(out=gh_bias[:, 0, :], in0=ghT[:, 0, :], scalar1=bias_r)
            nc.vector.tensor_scalar_add(out=gh_bias[:, 1, :], in0=ghT[:, 1, :], scalar1=bias_z)

        small_cast()
        small_transposes()
        small_finish()

        acc = [acc_pool.tile([P, ROWS], F32, name="acc%d" % gate) for gate in range(GATES)]

        sorted_tiles = {}
        bank_tiles = {}
        code_tiles = {}

        def sort_words(r):
            c = LOAD_OF_ROUND[r]
            raw32 = raws[c][:].bitcast(F32)
            lo = (r - LOAD_START[c]) * ROUND * WORDS
            srt = stage.tile([P, T, ROUND, HALVES, P], F32)
            nc.vector.tensor_copy(
                out=srt[:],
                in_=raw32[:, :, lo : lo + ROUND * WORDS].rearrange("b t (g p u) -> b t g u p", g=ROUND, u=HALVES),
            )
            sorted_tiles[r] = srt

        def transposes(r):
            srt = sorted_tiles[r]
            banks = []
            for g in range(ROUND):
                for pair in range(T // 2):
                    xt = xt_pool.tile([P, 2 * HALVES, B], F32, tag="xt")
                    for t in range(2):
                        for u in range(HALVES):
                            nc.tensor.transpose(
                                out=xt[:, t * HALVES + u, :], in_=srt[:, 2 * pair + t, g, u, :], identity=ident[:]
                            )
                    banks.append(xt)
            bank_tiles[r] = banks

        def quantise(r):
            grouped = stage.tile([P, ROUND, ROWS * PACK], BF16, align_bytes=64)
            codes = stage.tile([P, ROUND, ROWS], U32, align_bytes=64)
            x_planes = stage.tile([P, ROUND, ROWS], U8, align_bytes=64)
            grouped32 = grouped[:].bitcast(F32)
            span = 2 * B * HALVES
            for g in range(ROUND):
                for pair in range(T // 2):
                    nc.scalar.copy(
                        out=grouped32[:, g, pair * span : (pair + 1) * span].rearrange(
                            "p (t b u) -> p t b u", t=2, u=HALVES
                        ),
                        in_=bank_tiles[r][g * (T // 2) + pair][:].rearrange("p (t u) b -> p t b u", u=HALVES),
                    )
                nc.vector.quantize_mx(
                    out=codes[:, g, :].bitcast(FP8X4), scales=x_planes[:, g, :], in_=grouped[:, g, :]
                )
            code_tiles[r] = (codes, x_planes)

        def passes(r):
            codes, x_planes = code_tiles[r]
            for gate in range(GATES):
                cols = slice(gate * H, (gate + 1) * H)
                for g in range(ROUND):
                    k_pass = r * ROUND + g
                    nc.tensor.matmul_mx(
                        out=acc[gate][:],
                        lhsT=w_tiles[r // W_ROUNDS][:, k_pass % (W_ROUNDS * ROUND), cols].bitcast(FP8X4),
                        lhsT_scale=w_planes[:, k_pass, cols],
                        rhs=codes[:, g, :].bitcast(FP8X4),
                        rhs_scale=x_planes[:, g, :],
                        start=(k_pass == 0),
                        stop=(k_pass == PASSES - 1),
                    )

        def sort_and_refill(r):
            sort_words(r)
            issue_loads(r + 1)

        for r in range(SORT_AHEAD):
            sort_and_refill(r)
        for r in range(ROUNDS):
            if r + SORT_AHEAD < ROUNDS:
                sort_and_refill(r + SORT_AHEAD)
            transposes(r)
            quantise(r)
            if r > 0:
                passes(r - 1)
        passes(ROUNDS - 1)

        pieces = range(T // STEPS)

        def sums(gate, piece):
            return acc[gate][:, piece * STEPS * B : (piece + 1) * STEPS * B].rearrange("p (t b) -> p t b", t=STEPS)

        def every_step(ap):
            return ap.unsqueeze(1).to_broadcast([P, STEPS, B])

        tail_all = raw_pool.tile([P, TAIL_TILES, STEPS, B], F32, tag="raw3", bufs=RAW_BUFS[3])
        tail_used = []

        def tail_tiles(name):
            tiles = []
            for piece in pieces:
                tiles.append(tail_all[:, len(tail_used), :, :])
                tail_used.append(name)
            return tiles

        pre_r, r_gate, pre_z, one_minus_z = tail_tiles("pre_r"), tail_tiles("r_gate"), tail_tiles("pre_z"), tail_tiles("omz")
        r_hn, pre_n, n_gate, omz_rows, h_out = (
            tail_tiles("r_hn"), tail_tiles("pre_n"), tail_tiles("n_gate"), tail_tiles("omz_rows"), tail_tiles("h_out")
        )

        def to_rows(values):
            rows = xt_pool.tile([P, STEPS, H], F32, tag="xt")
            for t in range(STEPS):
                nc.tensor.transpose(out=rows[:, t, :], in_=values[:, t, :], identity=ident[:])
            return rows

        for i in pieces:
            nc.vector.tensor_tensor(out=pre_r[i][:], in0=sums(0, i), in1=every_step(gh_bias[:, 0, :]), op=ADD)
            nc.scalar.activation(out=r_gate[i][:], in_=pre_r[i][:], func=SIGMOID)
        for i in pieces:
            nc.vector.tensor_tensor(out=pre_z[i][:], in0=sums(1, i), in1=every_step(gh_bias[:, 1, :]), op=ADD)
            nc.scalar.activation(out=one_minus_z[i][:], in_=pre_z[i][:], func=SIGMOID, scale=-1.0)
        omz_banks = [to_rows(one_minus_z[i]) for i in pieces]
        for i in pieces:
            nc.vector.tensor_tensor(out=r_hn[i][:], in0=r_gate[i][:], in1=every_step(ghT[:, 2, :]), op=MULT)
            nc.vector.tensor_tensor(out=pre_n[i][:], in0=sums(2, i), in1=r_hn[i][:], op=ADD)
            nc.scalar.activation(out=n_gate[i][:], in_=pre_n[i][:], func=TANH, bias=bias_n)
        nc.vector.tensor_copy(out=omz_rows[0][:], in_=omz_banks[0][:])
        nc.scalar.copy(out=omz_rows[1][:], in_=omz_banks[1][:])
        for i in pieces:
            n_rows = to_rows(n_gate[i])
            nc.vector.tensor_tensor(out=h_out[i][:], in0=n_rows[:], in1=omz_rows[i][:], op=MULT)
            nc.sync.dma_start(out=out[:, i * STEPS : (i + 1) * STEPS, :], in_=h_out[i][:])
